import numpy as np
import ml_dtypes


def mxq(x, axis, fmt="e4m3"):
    dtype, down = {"e4m3": (ml_dtypes.float8_e4m3fn, 7), "e5m2": (ml_dtypes.float8_e5m2, 14)}[fmt]
    v = np.moveaxis(np.asarray(x, np.float32).astype(ml_dtypes.bfloat16).astype(np.float64), axis, -1)
    blocks = v.reshape(v.shape[:-1] + (-1, 32))
    amax = np.abs(blocks).max(-1, keepdims=True)
    byte = np.maximum(np.where(amax > 0, np.frexp(amax)[1] - 1 + 127, 0) - down, 1)
    scale = np.exp2(byte - 127.0)
    codes = (blocks / scale).astype(np.float32).astype(dtype).astype(np.float64)
    return np.moveaxis((codes * scale).reshape(v.shape), -1, axis)


WIDE = False


def mx_kscale(k):
    if not WIDE:
        return np.ones(k)
    levels = np.array([10, -10, 5, -5, 0])
    a = np.random.permutation(np.resize(levels, k // 512 * 4)).reshape(k // 512, 4)
    idx = np.arange(k)
    return np.exp2(a[idx // 512, idx % 128 // 32])


BF16 = ml_dtypes.bfloat16


def bf(x):
    return np.asarray(x, np.float32).astype(BF16)


def f64(x):
    return np.asarray(x).astype(np.float64)


K, D, H, R, V, B, T = 4, 1024, 256, 1024, 2052, 4, 1024
LN_EPS = 1e-5
ERF_CAP = 6.0
ERF_TERMS = 100


def erf(v):
    a = np.minimum(np.abs(v), ERF_CAP)
    term = a.copy()
    total = a.copy()
    for n in range(ERF_TERMS):
        term = term * (a * a) / (n + 1.5)
        total = total + term
    return np.sign(v) * total * np.exp(-a * a) / np.sqrt(0.25 * np.pi)


def gelu(v):
    return 0.5 * v * (1.0 + erf(v * np.sqrt(0.5)))


def setup_inputs():
    s = mx_kscale(D)
    amp = np.exp2(-9.0 * np.random.random((B, T, 1)))
    x = amp * (np.random.standard_normal((B, T, D)) + 0.5 * np.random.standard_normal((B, T, 1)))
    return {"x": bf(x),
            "ln_scale": bf((1.0 + 0.2 * np.random.standard_normal((K, D))) * s),
            "ln_bias": bf(0.2 * np.random.standard_normal((K, D)) * s),
            "W1": bf(np.random.standard_normal((K, D, H)) / np.sqrt(D) / s[None, :, None]),
            "b1": bf(0.3 * np.random.standard_normal((K, H)))}


def reference(x, ln_scale, ln_bias, W1, b1):
    x = f64(x)
    mu = x.mean(-1, keepdims=True)
    var = np.square(x - mu).mean(-1, keepdims=True)
    xn = (x - mu) / np.sqrt(var + LN_EPS)
    y = xn[:, None, :, :] * f64(ln_scale)[None, :, None, :] + f64(ln_bias)[None, :, None, :]
    return gelu((mxq(y, 3, "e4m3") @ mxq(f64(W1), 1, "e4m3")) + f64(b1)[None, :, None, :])

@@ -1,0 +1,183 @@
+from contextlib import ExitStack
+
+import concourse.mybir as mybir
+from concourse.masks import make_identity
+
+F32 = mybir.dt.float32
+BF16 = mybir.dt.bfloat16
+U32 = mybir.dt.uint32
+U8 = mybir.dt.uint8
+FP8X4 = mybir.dt.float8_e4m3fn_x4
+ACT = mybir.ActivationFunctionType
+ALU = mybir.AluOpType
+
+HEADS = 4
+D = 1024
+H = 256
+B = 4
+T = 1024
+LN_EPS = 1e-5
+P = 128
+PACK = 4
+PASSES = D // (P * PACK)
+D_BLOCKS = D // P
+TILES = 4
+GROUP = TILES * P
+GROUPS = B * T // GROUP
+BN_CHUNK = 512
+BN_CHUNKS = D // BN_CHUNK
+BN_DIM = 6
+
+FLOPS = 2 * B * HEADS * T * D * H
+
+
+def regroup(nc, grouped, planes):
+    nc.vector.tensor_copy(
+        out=grouped.rearrange("p (a i) t -> p a t i", i=4),
+        in_=planes.rearrange("p t (a i) -> p a t i", i=4),
+    )
+
+
+def quantise(nc, codes, scales, grouped):
+    nc.vector.quantize_mx(out=codes.bitcast(FP8X4), scales=scales, in_=grouped.rearrange("p w t -> p (w t)"))
+
+
+def tile_twostepvoicecraftheads_pa_t_kernel(tc, x, ln_scale, ln_bias, W1, b1, out):
+    nc = tc.nc
+    x_rows = x.flatten_outer_dims()
+
+    with ExitStack() as ctx:
+        const = ctx.enter_context(tc.tile_pool(name="const", bufs=1))
+        w_stage = ctx.enter_context(tc.tile_pool(name="w_stage", bufs=2))
+        x_pool = ctx.enter_context(tc.tile_pool(name="x_pool", bufs=3))
+        xn_pool = ctx.enter_context(tc.tile_pool(name="xn_pool", bufs=2))
+        stat_pool = ctx.enter_context(tc.tile_pool(name="stat_pool", bufs=3))
+        plane_pool = ctx.enter_context(tc.tile_pool(name="plane_pool", bufs=2 * HEADS))
+        grouped_pool = ctx.enter_context(tc.tile_pool(name="grouped_pool", bufs=3))
+        y_pool = ctx.enter_context(tc.tile_pool(name="y_pool", bufs=2 * HEADS))
+        res_pool = ctx.enter_context(tc.tile_pool(name="res_pool", bufs=2 * HEADS))
+        xt_psum = ctx.enter_context(tc.psum_pool(name="xt_psum", bufs=4))
+        acc_psum = ctx.enter_context(tc.psum_pool(name="acc_psum", bufs=4))
+
+        ident = const.tile([P, P], F32)
+        make_identity(nc, ident[:])
+        neg_half = const.tile([P, TILES], F32)
+        nc.vector.memset(neg_half[:], -0.5)
+
+        affine_rows_bf = const.tile([P, P], BF16)
+        nc.vector.memset(affine_rows_bf[:], 0.0)
+        n_rows = HEADS * D_BLOCKS
+        nc.scalar.dma_start(out=affine_rows_bf[0:n_rows, :], in_=ln_scale.rearrange("k (j p) -> (k j) p", p=P))
+        nc.scalar.dma_start(out=affine_rows_bf[n_rows : 2 * n_rows, :], in_=ln_bias.rearrange("k (j p) -> (k j) p", p=P))
+        affine_rows = const.tile([P, P], F32)
+        nc.vector.tensor_copy(out=affine_rows[:], in_=affine_rows_bf[:])
+        affine_cols_ps = xt_psum.tile([P, P], F32, tag="xt")
+        nc.tensor.transpose(affine_cols_ps[:], affine_rows[:], ident[:])
+        affine_cols = const.tile([P, P], F32)
+        nc.vector.tensor_copy(out=affine_cols[:], in_=affine_cols_ps[:])
+
+        b1_all = const.tile([P, HEADS, H], BF16)
+        nc.scalar.dma_start(
+            out=b1_all[:].rearrange("p k h -> p (k h)"),
+            in_=b1.rearrange("k h -> (k h)").partition_broadcast(P),
+        )
+
+        w_codes = const.tile([P, HEADS, PASSES * H], U32, align_bytes=64)
+        w_scales = const.tile([P, HEADS, PASSES * H], U8, align_bytes=64)
+        for head in range(HEADS):
+            w_raw = w_stage.tile([P, D_BLOCKS, H], BF16)
+            nc.scalar.dma_start(out=w_raw[:], in_=W1[head].rearrange("(j p) h -> p j h", p=P))
+            w_grouped = w_stage.tile([P, PASSES, H, PACK], BF16, align_bytes=64)
+            for c in range(PASSES):
+                regroup(nc, w_grouped[:, c], w_raw[:, c * PACK : (c + 1) * PACK, :])
+            quantise(nc, w_codes[:, head, :], w_scales[:, head, :], w_grouped[:].rearrange("p c h t -> p (c h) t"))
+
+        for g in range(GROUPS):
+            x_sb = x_pool.tile([P, TILES, D], BF16)
+            nc.sync.dma_start(
+                out=x_sb[:],
+                in_=x_rows[g * GROUP : (g + 1) * GROUP, :].rearrange("(p j) d -> p j d", j=TILES),
+            )
+
+            stats = stat_pool.tile([P, TILES, BN_CHUNKS * BN_DIM], F32)
+            mean_var = stat_pool.tile([P, TILES, 2], F32)
+            for j in range(TILES):
+                for s in range(BN_CHUNKS):
+                    nc.vector.bn_stats(
+                        out=stats[:, j, s * BN_DIM : (s + 1) * BN_DIM],
+                        in_=x_sb[:, j, s * BN_CHUNK : (s + 1) * BN_CHUNK],
+                    )
+                nc.vector.bn_aggr(out=mean_var[:, j, :], in_=stats[:, j, :])
+            var_eps = stat_pool.tile([P, TILES], F32)
+            nc.gpsimd.tensor_scalar(
+                out=var_eps[:], in0=mean_var[:, :, 1], scalar1=1.0, scalar2=LN_EPS, op0=ALU.mult, op1=ALU.add
+            )
+            rstd = stat_pool.tile([P, TILES], F32)
+            nc.gpsimd.tensor_tensor(out=rstd[:], in0=var_eps[:], in1=neg_half[:], op=ALU.pow)
+
+            xn = xn_pool.tile([P, TILES, D], F32)
+            for j in range(TILES):
+                nc.vector.tensor_scalar(
+                    out=xn[:, j, :],
+                    in0=x_sb[:, j, :],
+                    scalar1=mean_var[:, j, 0:1],
+                    scalar2=rstd[:, j : j + 1],
+                    op0=ALU.subtract,
+                    op1=ALU.mult,
+                )
+
+            y_codes = [y_pool.tile([P, PASSES, GROUP], U32, align_bytes=64, name="y_codes") for head in range(HEADS)]
+            y_scales = [y_pool.tile([P, PASSES, GROUP], U8, align_bytes=64, name="y_scales") for head in range(HEADS)]
+            for c in range(PASSES):
+                planes = [plane_pool.tile([P, PACK, GROUP], BF16, name="planes") for head in range(HEADS)]
+                for t in range(PACK):
+                    block = c * PACK + t
+                    xt = xt_psum.tile([P, GROUP], F32, tag="xt")
+                    for j in range(TILES):
+                        nc.tensor.transpose(xt[:, j * P : (j + 1) * P], xn[:, j, block * P : (block + 1) * P], ident[:])
+                    for head in range(HEADS):
+                        col = head * D_BLOCKS + block
+                        nc.scalar.activation(
+                            out=planes[head][:, t, :],
+                            in_=xt[:],
+                            func=ACT.Identity,
+                            scale=affine_cols[:, col : col + 1],
+                            bias=affine_cols[:, n_rows + col : n_rows + col + 1],
+                        )
+                grouped = {}
+                for head in range(HEADS):
+                    grouped[head] = grouped_pool.tile([P, GROUP, PACK], BF16, align_bytes=64, name="grouped")
+                    regroup(nc, grouped[head][:], planes[head][:])
+                    if head > 0:
+                        quantise(nc, y_codes[head - 1][:, c, :], y_scales[head - 1][:, c, :], grouped[head - 1][:])
+                quantise(nc, y_codes[HEADS - 1][:, c, :], y_scales[HEADS - 1][:, c, :], grouped[HEADS - 1][:])
+
+            batch, t0 = divmod(g * GROUP, T)
+            for head in range(HEADS):
+                res = res_pool.tile([P, TILES, H], F32)
+                for pair in range(TILES // 2):
+                    acc = acc_psum.tile([P, 2, H], F32)
+                    for half in range(2):
+                        j = 2 * pair + half
+                        for c in range(PASSES):
+                            nc.tensor.matmul_mx(
+                                out=acc[:, half, :],
+                                lhsT=y_codes[head][:, c, j * P : (j + 1) * P].bitcast(FP8X4),
+                                lhsT_scale=y_scales[head][:, c, j * P : (j + 1) * P],
+                                rhs=w_codes[:, head, c * H : (c + 1) * H].bitcast(FP8X4),
+                                rhs_scale=w_scales[:, head, c * H : (c + 1) * H],
+                                start=(c == 0),
+                                stop=(c == PASSES - 1),
+                            )
+                    res_pair = res[:, 2 * pair : 2 * pair + 2, :]
+                    nc.vector.tensor_tensor(
+                        out=res_pair,
+                        in0=acc[:],
+                        in1=b1_all[:, head, :].unsqueeze(1).to_broadcast([P, 2, H]),
+                        op=ALU.add,
+                    )
+                    nc.scalar.activation(out=res_pair, in_=res_pair, func=ACT.Gelu)
+                nc.sync.dma_start(
+                    out=out[batch, head, t0 : t0 + GROUP, :].rearrange("(p j) h -> p j h", j=TILES),
+                    in_=res[:],
+                )

@@ -28,6 +28,9 @@ BN_CHUNK = 512
 BN_CHUNKS = D // BN_CHUNK
 BN_DIM = 6
 
+STEPS = GROUPS * PASSES
+K_PASS = P * PACK
+
 FLOPS = 2 * B * HEADS * T * D * H
 
 
@@ -47,6 +50,7 @@ def tile_twostepvoicecraftheads_pa_t_kernel(tc, x, ln_scale, ln_bias, W1, b1, ou
     x_rows = x.flatten_outer_dims()
 
     with ExitStack() as ctx:
+        ctx.enter_context(tc.manual_schedule())
         const = ctx.enter_context(tc.tile_pool(name="const", bufs=1))
         w_stage = ctx.enter_context(tc.tile_pool(name="w_stage", bufs=2))
         x_pool = ctx.enter_context(tc.tile_pool(name="x_pool", bufs=3))
@@ -56,8 +60,129 @@ def tile_twostepvoicecraftheads_pa_t_kernel(tc, x, ln_scale, ln_bias, W1, b1, ou
         grouped_pool = ctx.enter_context(tc.tile_pool(name="grouped_pool", bufs=3))
         y_pool = ctx.enter_context(tc.tile_pool(name="y_pool", bufs=2 * HEADS))
         res_pool = ctx.enter_context(tc.tile_pool(name="res_pool", bufs=2 * HEADS))
-        xt_psum = ctx.enter_context(tc.psum_pool(name="xt_psum", bufs=4))
+        xt_psum = ctx.enter_context(tc.psum_pool(name="xt_psum", bufs=PACK))
         acc_psum = ctx.enter_context(tc.psum_pool(name="acc_psum", bufs=4))
+
+        x_sb, neg_mean, rstd, xn, xt, planes, y_codes, y_scales, res = {}, {}, {}, {}, {}, {}, {}, {}, {}
+
+        def load(g):
+            x_sb[g] = x_pool.tile([P, TILES, D], BF16, name="x_sb")
+            nc.sync.dma_start(
+                out=x_sb[g][:],
+                in_=x_rows[g * GROUP : (g + 1) * GROUP, :].rearrange("(p j) d -> p j d", j=TILES),
+            )
+
+        def statistics(g):
+            stats = stat_pool.tile([P, TILES, BN_CHUNKS * BN_DIM], F32)
+            mean_var = stat_pool.tile([P, TILES, 2], F32)
+            for j in range(TILES):
+                for s in range(BN_CHUNKS):
+                    nc.vector.bn_stats(
+                        out=stats[:, j, s * BN_DIM : (s + 1) * BN_DIM],
+                        in_=x_sb[g][:, j, s * BN_CHUNK : (s + 1) * BN_CHUNK],
+                    )
+                nc.vector.bn_aggr(out=mean_var[:, j, :], in_=stats[:, j, :])
+            var_eps = stat_pool.tile([P, TILES], F32)
+            nc.gpsimd.tensor_scalar(
+                out=var_eps[:], in0=mean_var[:, :, 1], scalar1=1.0, scalar2=LN_EPS, op0=ALU.mult, op1=ALU.add
+            )
+            rstd[g] = stat_pool.tile([P, TILES], F32, name="rstd")
+            nc.gpsimd.tensor_tensor(out=rstd[g][:], in0=var_eps[:], in1=neg_half[:], op=ALU.pow)
+            neg_mean[g] = stat_pool.tile([P, TILES], F32, name="neg_mean")
+            nc.gpsimd.tensor_scalar(
+                out=neg_mean[g][:], in0=mean_var[:, :, 0], scalar1=-1.0, scalar2=0.0, op0=ALU.mult, op1=ALU.add
+            )
+
+        def normalise(g):
+            xn[g] = xn_pool.tile([P, TILES, D], F32, name="xn")
+            for c in range(PASSES):
+                for j in range(TILES):
+                    nc.gpsimd.tensor_scalar(
+                        out=xn[g][:, j, c * K_PASS : (c + 1) * K_PASS],
+                        in0=x_sb[g][:, j, c * K_PASS : (c + 1) * K_PASS],
+                        scalar1=neg_mean[g][:, j : j + 1],
+                        scalar2=rstd[g][:, j : j + 1],
+                        op0=ALU.add,
+                        op1=ALU.mult,
+                    )
+
+        def transpose(step, t):
+            g, c = divmod(step, PASSES)
+            block = c * PACK + t
+            xt[step, t] = xt_psum.tile([P, GROUP], F32, name="xt")
+            for j in range(TILES):
+                nc.tensor.transpose(
+                    xt[step, t][:, j * P : (j + 1) * P], xn[g][:, j, block * P : (block + 1) * P], ident[:]
+                )
+
+        def affine(step, t):
+            block = (step % PASSES) * PACK + t
+            for head in range(HEADS):
+                if t == 0:
+                    planes[step, head] = plane_pool.tile([P, PACK, GROUP], BF16, name="planes")
+                col = head * D_BLOCKS + block
+                nc.scalar.activation(
+                    out=planes[step, head][:, t, :],
+                    in_=xt[step, t][:],
+                    func=ACT.Identity,
+                    scale=affine_cols[:, col : col + 1],
+                    bias=affine_cols[:, n_rows + col : n_rows + col + 1],
+                )
+
+        def pack(step):
+            g, c = divmod(step, PASSES)
+            grouped = {}
+            for head in range(HEADS):
+                if c == 0:
+                    y_codes[g, head] = y_pool.tile([P, PASSES, GROUP], U32, align_bytes=64, name="y_codes")
+                    y_scales[g, head] = y_pool.tile([P, PASSES, GROUP], U8, align_bytes=64, name="y_scales")
+                grouped[head] = grouped_pool.tile([P, GROUP, PACK], BF16, align_bytes=64, name="grouped")
+                regroup(nc, grouped[head][:], planes[step, head][:])
+                if head > 0:
+                    quantise(nc, y_codes[g, head - 1][:, c, :], y_scales[g, head - 1][:, c, :], grouped[head - 1][:])
+            quantise(nc, y_codes[g, HEADS - 1][:, c, :], y_scales[g, HEADS - 1][:, c, :], grouped[HEADS - 1][:])
+
+        def project(g, head):
+            res[g, head] = res_pool.tile([P, TILES, H], F32, name="res")
+            for pair in range(TILES // 2):
+                acc = acc_psum.tile([P, 2, H], F32)
+                for half in range(2):
+                    j = 2 * pair + half
+                    for c in range(PASSES):
+                        nc.tensor.matmul_mx(
+                            out=acc[:, half, :],
+                            lhsT=y_codes[g, head][:, c, j * P : (j + 1) * P].bitcast(FP8X4),
+                            lhsT_scale=y_scales[g, head][:, c, j * P : (j + 1) * P],
+                            rhs=w_codes[:, head, c * H : (c + 1) * H].bitcast(FP8X4),
+                            rhs_scale=w_scales[:, head, c * H : (c + 1) * H],
+                            start=(c == 0),
+                            stop=(c == PASSES - 1),
+                        )
+                nc.vector.tensor_tensor(
+                    out=res[g, head][:, 2 * pair : 2 * pair + 2, :],
+                    in0=acc[:],
+                    in1=b1_all[:, head, :].unsqueeze(1).to_broadcast([P, 2, H]),
+                    op=ALU.add,
+                )
+
+        def gelu(g, head, pair):
+            res_pair = res[g, head][:, 2 * pair : 2 * pair + 2, :]
+            nc.scalar.activation(out=res_pair, in_=res_pair, func=ACT.Gelu)
+
+        def store(g, head):
+            batch, t0 = divmod(g * GROUP, T)
+            nc.sync.dma_start(
+                out=out[batch, head, t0 : t0 + GROUP, :].rearrange("(p j) h -> p j h", j=TILES),
+                in_=res[g, head][:],
+            )
+
+        load(0)
+        w_raw = {}
+        for head in range(HEADS):
+            w_raw[head] = w_stage.tile([P, D_BLOCKS, H], BF16, name="w_raw", bufs=HEADS)
+            nc.sync.dma_start(out=w_raw[head][:], in_=W1[head].rearrange("(j p) h -> p j h", p=P))
+        load(1)
+        load(2)
 
         ident = const.tile([P, P], F32)
         make_identity(nc, ident[:])
@@ -82,102 +207,39 @@ def tile_twostepvoicecraftheads_pa_t_kernel(tc, x, ln_scale, ln_bias, W1, b1, ou
             in_=b1.rearrange("k h -> (k h)").partition_broadcast(P),
         )
 
+        statistics(0)
+        normalise(0)
+        for t in range(PACK):
+            transpose(0, t)
         w_codes = const.tile([P, HEADS, PASSES * H], U32, align_bytes=64)
         w_scales = const.tile([P, HEADS, PASSES * H], U8, align_bytes=64)
         for head in range(HEADS):
-            w_raw = w_stage.tile([P, D_BLOCKS, H], BF16)
-            nc.scalar.dma_start(out=w_raw[:], in_=W1[head].rearrange("(j p) h -> p j h", p=P))
             w_grouped = w_stage.tile([P, PASSES, H, PACK], BF16, align_bytes=64)
             for c in range(PASSES):
-                regroup(nc, w_grouped[:, c], w_raw[:, c * PACK : (c + 1) * PACK, :])
+                regroup(nc, w_grouped[:, c], w_raw[head][:, c * PACK : (c + 1) * PACK, :])
             quantise(nc, w_codes[:, head, :], w_scales[:, head, :], w_grouped[:].rearrange("p c h t -> p (c h) t"))
+        statistics(1)
+        normalise(1)
 
-        for g in range(GROUPS):
-            x_sb = x_pool.tile([P, TILES, D], BF16)
-            nc.sync.dma_start(
-                out=x_sb[:],
-                in_=x_rows[g * GROUP : (g + 1) * GROUP, :].rearrange("(p j) d -> p j d", j=TILES),
-            )
-
-            stats = stat_pool.tile([P, TILES, BN_CHUNKS * BN_DIM], F32)
-            mean_var = stat_pool.tile([P, TILES, 2], F32)
-            for j in range(TILES):
-                for s in range(BN_CHUNKS):
-                    nc.vector.bn_stats(
-                        out=stats[:, j, s * BN_DIM : (s + 1) * BN_DIM],
-                        in_=x_sb[:, j, s * BN_CHUNK : (s + 1) * BN_CHUNK],
-                    )
-                nc.vector.bn_aggr(out=mean_var[:, j, :], in_=stats[:, j, :])
-            var_eps = stat_pool.tile([P, TILES], F32)
-            nc.gpsimd.tensor_scalar(
-                out=var_eps[:], in0=mean_var[:, :, 1], scalar1=1.0, scalar2=LN_EPS, op0=ALU.mult, op1=ALU.add
-            )
-            rstd = stat_pool.tile([P, TILES], F32)
-            nc.gpsimd.tensor_tensor(out=rstd[:], in0=var_eps[:], in1=neg_half[:], op=ALU.pow)
-
-            xn = xn_pool.tile([P, TILES, D], F32)
-            for j in range(TILES):
-                nc.vector.tensor_scalar(
-                    out=xn[:, j, :],
-                    in0=x_sb[:, j, :],
-                    scalar1=mean_var[:, j, 0:1],
-                    scalar2=rstd[:, j : j + 1],
-                    op0=ALU.subtract,
-                    op1=ALU.mult,
-                )
-
-            y_codes = [y_pool.tile([P, PASSES, GROUP], U32, align_bytes=64, name="y_codes") for head in range(HEADS)]
-            y_scales = [y_pool.tile([P, PASSES, GROUP], U8, align_bytes=64, name="y_scales") for head in range(HEADS)]
-            for c in range(PASSES):
-                planes = [plane_pool.tile([P, PACK, GROUP], BF16, name="planes") for head in range(HEADS)]
-                for t in range(PACK):
-                    block = c * PACK + t
-                    xt = xt_psum.tile([P, GROUP], F32, tag="xt")
-                    for j in range(TILES):
-                        nc.tensor.transpose(xt[:, j * P : (j + 1) * P], xn[:, j, block * P : (block + 1) * P], ident[:])
-                    for head in range(HEADS):
-                        col = head * D_BLOCKS + block
-                        nc.scalar.activation(
-                            out=planes[head][:, t, :],
-                            in_=xt[:],
-                            func=ACT.Identity,
-                            scale=affine_cols[:, col : col + 1],
-                            bias=affine_cols[:, n_rows + col : n_rows + col + 1],
-                        )
-                grouped = {}
-                for head in range(HEADS):
-                    grouped[head] = grouped_pool.tile([P, GROUP, PACK], BF16, align_bytes=64, name="grouped")
-                    regroup(nc, grouped[head][:], planes[head][:])
-                    if head > 0:
-                        quantise(nc, y_codes[head - 1][:, c, :], y_scales[head - 1][:, c, :], grouped[head - 1][:])
-                quantise(nc, y_codes[HEADS - 1][:, c, :], y_scales[HEADS - 1][:, c, :], grouped[HEADS - 1][:])
-
-            batch, t0 = divmod(g * GROUP, T)
-            for head in range(HEADS):
-                res = res_pool.tile([P, TILES, H], F32)
-                for pair in range(TILES // 2):
-                    acc = acc_psum.tile([P, 2, H], F32)
-                    for half in range(2):
-                        j = 2 * pair + half
-                        for c in range(PASSES):
-                            nc.tensor.matmul_mx(
-                                out=acc[:, half, :],
-                                lhsT=y_codes[head][:, c, j * P : (j + 1) * P].bitcast(FP8X4),
-                                lhsT_scale=y_scales[head][:, c, j * P : (j + 1) * P],
-                                rhs=w_codes[:, head, c * H : (c + 1) * H].bitcast(FP8X4),
-                                rhs_scale=w_scales[:, head, c * H : (c + 1) * H],
-                                start=(c == 0),
-                                stop=(c == PASSES - 1),
-                            )
-                    res_pair = res[:, 2 * pair : 2 * pair + 2, :]
-                    nc.vector.tensor_tensor(
-                        out=res_pair,
-                        in0=acc[:],
-                        in1=b1_all[:, head, :].unsqueeze(1).to_broadcast([P, 2, H]),
-                        op=ALU.add,
-                    )
-                    nc.scalar.activation(out=res_pair, in_=res_pair, func=ACT.Gelu)
-                nc.sync.dma_start(
-                    out=out[batch, head, t0 : t0 + GROUP, :].rearrange("(p j) h -> p j h", j=TILES),
-                    in_=res[:],
-                )
+        for step in range(STEPS + 3):
+            g, c = divmod(step, PASSES)
+            if 1 <= step <= STEPS:
+                pack(step - 1)
+            for t in range(PACK):
+                if step < STEPS:
+                    affine(step, t)
+                if c == 0 and 1 <= g <= GROUPS:
+                    project(g - 1, t)
+                if step + 1 < STEPS:
+                    transpose(step + 1, t)
+                done_g, done_half = divmod(step - 3, 2)
+                if 0 <= done_g < GROUPS:
+                    head, pair = 2 * done_half + t // 2, t % 2
+                    gelu(done_g, head, pair)
+                    if pair == 1:
+                        store(done_g, head)
+            if c == 1 and g + 2 < GROUPS:
+                if g + 3 < GROUPS:
+                    load(g + 3)
+                statistics(g + 2)
+                normalise(g + 2)

@@ -29,7 +29,12 @@ BN_CHUNKS = D // BN_CHUNK
 BN_DIM = 6
 
 STEPS = GROUPS * PASSES
-K_PASS = P * PACK
+ROUND_HEADS = 2
+STEP_ROUNDS = HEADS // ROUND_HEADS
+ROUNDS = STEPS * STEP_ROUNDS
+STAT_LEAD = 6
+PROJECT_LAG = 4
+GELU_LAG = PROJECT_LAG + 1
 
 FLOPS = 2 * B * HEADS * T * D * H
 
@@ -55,56 +60,46 @@ def tile_twostepvoicecraftheads_pa_t_kernel(tc, x, ln_scale, ln_bias, W1, b1, ou
         w_stage = ctx.enter_context(tc.tile_pool(name="w_stage", bufs=2))
         x_pool = ctx.enter_context(tc.tile_pool(name="x_pool", bufs=3))
         xn_pool = ctx.enter_context(tc.tile_pool(name="xn_pool", bufs=2))
-        stat_pool = ctx.enter_context(tc.tile_pool(name="stat_pool", bufs=3))
-        plane_pool = ctx.enter_context(tc.tile_pool(name="plane_pool", bufs=2 * HEADS))
+        stat_pool = ctx.enter_context(tc.tile_pool(name="stat_pool", bufs=4))
+        plane_pool = ctx.enter_context(tc.tile_pool(name="plane_pool", bufs=3 * ROUND_HEADS))
         grouped_pool = ctx.enter_context(tc.tile_pool(name="grouped_pool", bufs=3))
         y_pool = ctx.enter_context(tc.tile_pool(name="y_pool", bufs=2 * HEADS))
-        res_pool = ctx.enter_context(tc.tile_pool(name="res_pool", bufs=2 * HEADS))
+        res_pool = ctx.enter_context(tc.tile_pool(name="res_pool", bufs=4))
         xt_psum = ctx.enter_context(tc.psum_pool(name="xt_psum", bufs=PACK))
         acc_psum = ctx.enter_context(tc.psum_pool(name="acc_psum", bufs=4))
 
-        x_sb, neg_mean, rstd, xn, xt, planes, y_codes, y_scales, res = {}, {}, {}, {}, {}, {}, {}, {}, {}
+        x_sb, xn, xt, planes, y_codes, y_scales, res = {}, {}, {}, {}, {}, {}, {}
 
         def load(g):
             x_sb[g] = x_pool.tile([P, TILES, D], BF16, name="x_sb")
-            nc.sync.dma_start(
-                out=x_sb[g][:],
-                in_=x_rows[g * GROUP : (g + 1) * GROUP, :].rearrange("(p j) d -> p j d", j=TILES),
-            )
-
-        def statistics(g):
-            stats = stat_pool.tile([P, TILES, BN_CHUNKS * BN_DIM], F32)
-            mean_var = stat_pool.tile([P, TILES, 2], F32)
+            rows = x_rows[g * GROUP : (g + 1) * GROUP, :].rearrange("(p j) d -> p j d", j=TILES)
             for j in range(TILES):
-                for s in range(BN_CHUNKS):
-                    nc.vector.bn_stats(
-                        out=stats[:, j, s * BN_DIM : (s + 1) * BN_DIM],
-                        in_=x_sb[g][:, j, s * BN_CHUNK : (s + 1) * BN_CHUNK],
-                    )
-                nc.vector.bn_aggr(out=mean_var[:, j, :], in_=stats[:, j, :])
-            var_eps = stat_pool.tile([P, TILES], F32)
-            nc.gpsimd.tensor_scalar(
-                out=var_eps[:], in0=mean_var[:, :, 1], scalar1=1.0, scalar2=LN_EPS, op0=ALU.mult, op1=ALU.add
-            )
-            rstd[g] = stat_pool.tile([P, TILES], F32, name="rstd")
-            nc.gpsimd.tensor_tensor(out=rstd[g][:], in0=var_eps[:], in1=neg_half[:], op=ALU.pow)
-            neg_mean[g] = stat_pool.tile([P, TILES], F32, name="neg_mean")
-            nc.gpsimd.tensor_scalar(
-                out=neg_mean[g][:], in0=mean_var[:, :, 0], scalar1=-1.0, scalar2=0.0, op0=ALU.mult, op1=ALU.add
-            )
+                nc.sync.dma_start(out=x_sb[g][:, j, :], in_=rows[:, j, :])
 
-        def normalise(g):
-            xn[g] = xn_pool.tile([P, TILES, D], F32, name="xn")
-            for c in range(PASSES):
-                for j in range(TILES):
-                    nc.gpsimd.tensor_scalar(
-                        out=xn[g][:, j, c * K_PASS : (c + 1) * K_PASS],
-                        in0=x_sb[g][:, j, c * K_PASS : (c + 1) * K_PASS],
-                        scalar1=neg_mean[g][:, j : j + 1],
-                        scalar2=rstd[g][:, j : j + 1],
-                        op0=ALU.add,
-                        op1=ALU.mult,
-                    )
+        def normalise(g, j):
+            if j == 0:
+                xn[g] = xn_pool.tile([P, TILES, D], F32, name="xn")
+            stats = stat_pool.tile([P, BN_CHUNKS * BN_DIM], F32)
+            for s in range(BN_CHUNKS):
+                nc.vector.bn_stats(
+                    out=stats[:, s * BN_DIM : (s + 1) * BN_DIM],
+                    in_=x_sb[g][:, j, s * BN_CHUNK : (s + 1) * BN_CHUNK],
+                )
+            mean_var = stat_pool.tile([P, 2], F32)
+            nc.vector.bn_aggr(out=mean_var[:], in_=stats[:])
+            var_eps = stat_pool.tile([P, 1], F32)
+            nc.gpsimd.tensor_scalar(
+                out=var_eps[:], in0=mean_var[:, 1:2], scalar1=1.0, scalar2=LN_EPS, op0=ALU.mult, op1=ALU.add
+            )
+            rstd = stat_pool.tile([P, 1], F32)
+            nc.gpsimd.tensor_tensor(out=rstd[:], in0=var_eps[:], in1=neg_half[:], op=ALU.pow)
+            neg_mean = stat_pool.tile([P, 1], F32)
+            nc.gpsimd.tensor_scalar(
+                out=neg_mean[:], in0=mean_var[:, 0:1], scalar1=-1.0, scalar2=0.0, op0=ALU.mult, op1=ALU.add
+            )
+            nc.gpsimd.tensor_scalar(
+                out=xn[g][:, j, :], in0=x_sb[g][:, j, :], scalar1=neg_mean[:], scalar2=rstd[:], op0=ALU.add, op1=ALU.mult
+            )
 
         def transpose(step, t):
             g, c = divmod(step, PASSES)
@@ -115,32 +110,29 @@ def tile_twostepvoicecraftheads_pa_t_kernel(tc, x, ln_scale, ln_bias, W1, b1, ou
                     xt[step, t][:, j * P : (j + 1) * P], xn[g][:, j, block * P : (block + 1) * P], ident[:]
                 )
 
-        def affine(step, t):
-            block = (step % PASSES) * PACK + t
-            for head in range(HEADS):
-                if t == 0:
-                    planes[step, head] = plane_pool.tile([P, PACK, GROUP], BF16, name="planes")
-                col = head * D_BLOCKS + block
-                nc.scalar.activation(
-                    out=planes[step, head][:, t, :],
-                    in_=xt[step, t][:],
-                    func=ACT.Identity,
-                    scale=affine_cols[:, col : col + 1],
-                    bias=affine_cols[:, n_rows + col : n_rows + col + 1],
-                )
+        def affine(step, t, head):
+            if t == 0:
+                planes[step, head] = plane_pool.tile([P, PACK, GROUP], BF16, name="planes")
+            col = head * D_BLOCKS + (step % PASSES) * PACK + t
+            nc.scalar.activation(
+                out=planes[step, head][:, t, :],
+                in_=xt[step, t][:],
+                func=ACT.Identity,
+                scale=affine_cols[:, col : col + 1],
+                bias=affine_cols[:, n_rows + col : n_rows + col + 1],
+            )
 
-        def pack(step):
+        def pack(step, heads):
             g, c = divmod(step, PASSES)
             grouped = {}
-            for head in range(HEADS):
+            for head in heads:
                 if c == 0:
                     y_codes[g, head] = y_pool.tile([P, PASSES, GROUP], U32, align_bytes=64, name="y_codes")
                     y_scales[g, head] = y_pool.tile([P, PASSES, GROUP], U8, align_bytes=64, name="y_scales")
                 grouped[head] = grouped_pool.tile([P, GROUP, PACK], BF16, align_bytes=64, name="grouped")
                 regroup(nc, grouped[head][:], planes[step, head][:])
-                if head > 0:
-                    quantise(nc, y_codes[g, head - 1][:, c, :], y_scales[g, head - 1][:, c, :], grouped[head - 1][:])
-            quantise(nc, y_codes[g, HEADS - 1][:, c, :], y_scales[g, HEADS - 1][:, c, :], grouped[HEADS - 1][:])
+            for head in heads:
+                quantise(nc, y_codes[g, head][:, c, :], y_scales[g, head][:, c, :], grouped[head][:])
 
         def project(g, head):
             res[g, head] = res_pool.tile([P, TILES, H], F32, name="res")
@@ -176,39 +168,37 @@ def tile_twostepvoicecraftheads_pa_t_kernel(tc, x, ln_scale, ln_bias, W1, b1, ou
                 in_=res[g, head][:],
             )
 
+        n_rows = HEADS * D_BLOCKS
+        affine_rows_bf = const.tile([P, P], BF16)
+        nc.vector.memset(affine_rows_bf[:], 0.0)
+        nc.scalar.dma_start(out=affine_rows_bf[0:n_rows, :], in_=ln_scale.rearrange("k (j p) -> (k j) p", p=P))
+        nc.scalar.dma_start(out=affine_rows_bf[n_rows : 2 * n_rows, :], in_=ln_bias.rearrange("k (j p) -> (k j) p", p=P))
         load(0)
+        load(1)
         w_raw = {}
         for head in range(HEADS):
             w_raw[head] = w_stage.tile([P, D_BLOCKS, H], BF16, name="w_raw", bufs=HEADS)
             nc.sync.dma_start(out=w_raw[head][:], in_=W1[head].rearrange("(j p) h -> p j h", p=P))
-        load(1)
         load(2)
-
-        ident = const.tile([P, P], F32)
-        make_identity(nc, ident[:])
-        neg_half = const.tile([P, TILES], F32)
-        nc.vector.memset(neg_half[:], -0.5)
-
-        affine_rows_bf = const.tile([P, P], BF16)
-        nc.vector.memset(affine_rows_bf[:], 0.0)
-        n_rows = HEADS * D_BLOCKS
-        nc.scalar.dma_start(out=affine_rows_bf[0:n_rows, :], in_=ln_scale.rearrange("k (j p) -> (k j) p", p=P))
-        nc.scalar.dma_start(out=affine_rows_bf[n_rows : 2 * n_rows, :], in_=ln_bias.rearrange("k (j p) -> (k j) p", p=P))
-        affine_rows = const.tile([P, P], F32)
-        nc.vector.tensor_copy(out=affine_rows[:], in_=affine_rows_bf[:])
-        affine_cols_ps = xt_psum.tile([P, P], F32, tag="xt")
-        nc.tensor.transpose(affine_cols_ps[:], affine_rows[:], ident[:])
-        affine_cols = const.tile([P, P], F32)
-        nc.vector.tensor_copy(out=affine_cols[:], in_=affine_cols_ps[:])
-
         b1_all = const.tile([P, HEADS, H], BF16)
         nc.scalar.dma_start(
             out=b1_all[:].rearrange("p k h -> p (k h)"),
             in_=b1.rearrange("k h -> (k h)").partition_broadcast(P),
         )
 
-        statistics(0)
-        normalise(0)
+        ident = const.tile([P, P], F32)
+        make_identity(nc, ident[:])
+        neg_half = const.tile([P, 1], F32)
+        nc.vector.memset(neg_half[:], -0.5)
+        affine_rows = const.tile([P, P], F32)
+        nc.scalar.copy(out=affine_rows[:], in_=affine_rows_bf[:])
+        affine_cols_ps = xt_psum.tile([P, P], F32, tag="xt")
+        nc.tensor.transpose(affine_cols_ps[:], affine_rows[:], ident[:])
+        affine_cols = const.tile([P, P], F32)
+        nc.scalar.copy(out=affine_cols[:], in_=affine_cols_ps[:])
+
+        for n in range(STAT_LEAD):
+            normalise(n // TILES, n % TILES)
         for t in range(PACK):
             transpose(0, t)
         w_codes = const.tile([P, HEADS, PASSES * H], U32, align_bytes=64)
@@ -218,28 +208,26 @@ def tile_twostepvoicecraftheads_pa_t_kernel(tc, x, ln_scale, ln_bias, W1, b1, ou
             for c in range(PASSES):
                 regroup(nc, w_grouped[:, c], w_raw[head][:, c * PACK : (c + 1) * PACK, :])
             quantise(nc, w_codes[:, head, :], w_scales[:, head, :], w_grouped[:].rearrange("p c h t -> p (c h) t"))
-        statistics(1)
-        normalise(1)
 
-        for step in range(STEPS + 3):
-            g, c = divmod(step, PASSES)
-            if 1 <= step <= STEPS:
-                pack(step - 1)
+        for rnd in range(ROUNDS + GELU_LAG):
+            step, part = divmod(rnd, STEP_ROUNDS)
+            if 1 <= rnd <= ROUNDS:
+                last_step, last_part = divmod(rnd - 1, STEP_ROUNDS)
+                pack(last_step, range(last_part * ROUND_HEADS, (last_part + 1) * ROUND_HEADS))
+            n = rnd + STAT_LEAD
+            if n < GROUPS * TILES:
+                if n % TILES == 0 and n // TILES + 1 < GROUPS:
+                    load(n // TILES + 1)
+                normalise(n // TILES, n % TILES)
+            if 0 <= rnd - PROJECT_LAG < GROUPS * HEADS:
+                project((rnd - PROJECT_LAG) // HEADS, (rnd - PROJECT_LAG) % HEADS)
             for t in range(PACK):
-                if step < STEPS:
-                    affine(step, t)
-                if c == 0 and 1 <= g <= GROUPS:
-                    project(g - 1, t)
-                if step + 1 < STEPS:
-                    transpose(step + 1, t)
-                done_g, done_half = divmod(step - 3, 2)
-                if 0 <= done_g < GROUPS:
-                    head, pair = 2 * done_half + t // 2, t % 2
-                    gelu(done_g, head, pair)
-                    if pair == 1:
-                        store(done_g, head)
-            if c == 1 and g + 2 < GROUPS:
-                if g + 3 < GROUPS:
-                    load(g + 3)
-                statistics(g + 2)
-                normalise(g + 2)
+                if rnd < ROUNDS:
+                    for head in range(part * ROUND_HEADS, (part + 1) * ROUND_HEADS):
+                        affine(step, t, head)
+                    if part == STEP_ROUNDS - 1 and step + 1 < STEPS:
+                        transpose(step + 1, t)
+                if t % 2 == 1 and 0 <= rnd - GELU_LAG < GROUPS * HEADS:
+                    gelu((rnd - GELU_LAG) // HEADS, (rnd - GELU_LAG) % HEADS, t // 2)
+            if 0 <= rnd - GELU_LAG < GROUPS * HEADS:
+                store((rnd - GELU_LAG) // HEADS, (rnd - GELU_LAG) % HEADS)

@@ -29,12 +29,11 @@ BN_CHUNKS = D // BN_CHUNK
 BN_DIM = 6
 
 STEPS = GROUPS * PASSES
-ROUND_HEADS = 2
-STEP_ROUNDS = HEADS // ROUND_HEADS
-ROUNDS = STEPS * STEP_ROUNDS
-STAT_LEAD = 6
-PROJECT_LAG = 4
-GELU_LAG = PROJECT_LAG + 1
+PAIRS = TILES // 2
+FIRST_HEADS = (0, 1)
+LAST_HEADS = (2, 3)
+NORM_LEAD = 3
+STAT_LEAD = NORM_LEAD + 1
 
 FLOPS = 2 * B * HEADS * T * D * H
 
@@ -60,15 +59,15 @@ def tile_twostepvoicecraftheads_pa_t_kernel(tc, x, ln_scale, ln_bias, W1, b1, ou
         w_stage = ctx.enter_context(tc.tile_pool(name="w_stage", bufs=2))
         x_pool = ctx.enter_context(tc.tile_pool(name="x_pool", bufs=3))
         xn_pool = ctx.enter_context(tc.tile_pool(name="xn_pool", bufs=2))
-        stat_pool = ctx.enter_context(tc.tile_pool(name="stat_pool", bufs=4))
-        plane_pool = ctx.enter_context(tc.tile_pool(name="plane_pool", bufs=3 * ROUND_HEADS))
-        grouped_pool = ctx.enter_context(tc.tile_pool(name="grouped_pool", bufs=3))
+        stat_pool = ctx.enter_context(tc.tile_pool(name="stat_pool", bufs=3))
+        plane_pool = ctx.enter_context(tc.tile_pool(name="plane_pool", bufs=2 * HEADS))
+        grouped_pool = ctx.enter_context(tc.tile_pool(name="grouped_pool", bufs=4))
         y_pool = ctx.enter_context(tc.tile_pool(name="y_pool", bufs=2 * HEADS))
-        res_pool = ctx.enter_context(tc.tile_pool(name="res_pool", bufs=4))
+        res_pool = ctx.enter_context(tc.tile_pool(name="res_pool", bufs=6))
         xt_psum = ctx.enter_context(tc.psum_pool(name="xt_psum", bufs=PACK))
-        acc_psum = ctx.enter_context(tc.psum_pool(name="acc_psum", bufs=4))
+        acc_psum = ctx.enter_context(tc.psum_pool(name="acc_psum", bufs=2 * PAIRS))
 
-        x_sb, xn, xt, planes, y_codes, y_scales, res = {}, {}, {}, {}, {}, {}, {}
+        x_sb, stats, mean_var, rstd, xn, xt, planes, y_codes, y_scales, acc, res = {}, {}, {}, {}, {}, {}, {}, {}, {}, {}, {}
 
         def load(g):
             x_sb[g] = x_pool.tile([P, TILES, D], BF16, name="x_sb")
@@ -76,30 +75,43 @@ def tile_twostepvoicecraftheads_pa_t_kernel(tc, x, ln_scale, ln_bias, W1, b1, ou
             for j in range(TILES):
                 nc.sync.dma_start(out=x_sb[g][:, j, :], in_=rows[:, j, :])
 
-        def normalise(g, j):
-            if j == 0:
+        def sum_tokens(m):
+            g, pair = divmod(m, PAIRS)
+            stats[m] = stat_pool.tile([P, 2, BN_CHUNKS * BN_DIM], F32, name="stats")
+            for half in range(2):
+                for s in range(BN_CHUNKS):
+                    nc.vector.bn_stats(
+                        out=stats[m][:, half, s * BN_DIM : (s + 1) * BN_DIM],
+                        in_=x_sb[g][:, 2 * pair + half, s * BN_CHUNK : (s + 1) * BN_CHUNK],
+                    )
+
+        def mean_and_rstd(m):
+            mean_var[m] = stat_pool.tile([P, 2, 2], F32, name="mean_var")
+            for half in range(2):
+                nc.vector.bn_aggr(out=mean_var[m][:, half, :], in_=stats[m][:, half, :])
+            var_eps = stat_pool.tile([P, 2], F32)
+            nc.gpsimd.tensor_scalar(
+                out=var_eps[:], in0=mean_var[m][:, :, 1], scalar1=1.0, scalar2=LN_EPS, op0=ALU.mult, op1=ALU.add
+            )
+            rstd[m] = stat_pool.tile([P, 2], F32, name="rstd")
+            nc.gpsimd.tensor_tensor(out=rstd[m][:], in0=var_eps[:], in1=neg_half[:], op=ALU.pow)
+
+        def normalise(m):
+            g, pair = divmod(m, PAIRS)
+            if pair == 0:
                 xn[g] = xn_pool.tile([P, TILES, D], F32, name="xn")
-            stats = stat_pool.tile([P, BN_CHUNKS * BN_DIM], F32)
-            for s in range(BN_CHUNKS):
-                nc.vector.bn_stats(
-                    out=stats[:, s * BN_DIM : (s + 1) * BN_DIM],
-                    in_=x_sb[g][:, j, s * BN_CHUNK : (s + 1) * BN_CHUNK],
+            neg_mean = stat_pool.tile([P, 2], F32)
+            nc.vector.tensor_scalar_mul(out=neg_mean[:], in0=mean_var[m][:, :, 0], scalar1=-1.0)
+            for half in range(2):
+                j = 2 * pair + half
+                nc.gpsimd.tensor_scalar(
+                    out=xn[g][:, j, :],
+                    in0=x_sb[g][:, j, :],
+                    scalar1=neg_mean[:, half : half + 1],
+                    scalar2=rstd[m][:, half : half + 1],
+                    op0=ALU.add,
+                    op1=ALU.mult,
                 )
-            mean_var = stat_pool.tile([P, 2], F32)
-            nc.vector.bn_aggr(out=mean_var[:], in_=stats[:])
-            var_eps = stat_pool.tile([P, 1], F32)
-            nc.gpsimd.tensor_scalar(
-                out=var_eps[:], in0=mean_var[:, 1:2], scalar1=1.0, scalar2=LN_EPS, op0=ALU.mult, op1=ALU.add
-            )
-            rstd = stat_pool.tile([P, 1], F32)
-            nc.gpsimd.tensor_tensor(out=rstd[:], in0=var_eps[:], in1=neg_half[:], op=ALU.pow)
-            neg_mean = stat_pool.tile([P, 1], F32)
-            nc.gpsimd.tensor_scalar(
-                out=neg_mean[:], in0=mean_var[:, 0:1], scalar1=-1.0, scalar2=0.0, op0=ALU.mult, op1=ALU.add
-            )
-            nc.gpsimd.tensor_scalar(
-                out=xn[g][:, j, :], in0=x_sb[g][:, j, :], scalar1=neg_mean[:], scalar2=rstd[:], op0=ALU.add, op1=ALU.mult
-            )
 
         def transpose(step, t):
             g, c = divmod(step, PASSES)
@@ -134,15 +146,15 @@ def tile_twostepvoicecraftheads_pa_t_kernel(tc, x, ln_scale, ln_bias, W1, b1, ou
             for head in heads:
                 quantise(nc, y_codes[g, head][:, c, :], y_scales[g, head][:, c, :], grouped[head][:])
 
-        def project(g, head):
-            res[g, head] = res_pool.tile([P, TILES, H], F32, name="res")
-            for pair in range(TILES // 2):
-                acc = acc_psum.tile([P, 2, H], F32)
+        def project(u):
+            g, head = divmod(u, HEADS)
+            for pair in range(PAIRS):
+                acc[u, pair] = acc_psum.tile([P, 2, H], F32, name="acc")
                 for half in range(2):
                     j = 2 * pair + half
                     for c in range(PASSES):
                         nc.tensor.matmul_mx(
-                            out=acc[:, half, :],
+                            out=acc[u, pair][:, half, :],
                             lhsT=y_codes[g, head][:, c, j * P : (j + 1) * P].bitcast(FP8X4),
                             lhsT_scale=y_scales[g, head][:, c, j * P : (j + 1) * P],
                             rhs=w_codes[:, head, c * H : (c + 1) * H].bitcast(FP8X4),
@@ -150,22 +162,27 @@ def tile_twostepvoicecraftheads_pa_t_kernel(tc, x, ln_scale, ln_bias, W1, b1, ou
                             start=(c == 0),
                             stop=(c == PASSES - 1),
                         )
+
+        def add_bias(u):
+            res[u] = res_pool.tile([P, TILES, H], F32, name="res")
+            for pair in range(PAIRS):
                 nc.vector.tensor_tensor(
-                    out=res[g, head][:, 2 * pair : 2 * pair + 2, :],
-                    in0=acc[:],
-                    in1=b1_all[:, head, :].unsqueeze(1).to_broadcast([P, 2, H]),
+                    out=res[u][:, 2 * pair : 2 * pair + 2, :],
+                    in0=acc[u, pair][:],
+                    in1=b1_all[:, u % HEADS, :].unsqueeze(1).to_broadcast([P, 2, H]),
                     op=ALU.add,
                 )
 
-        def gelu(g, head, pair):
-            res_pair = res[g, head][:, 2 * pair : 2 * pair + 2, :]
+        def gelu(u, pair):
+            res_pair = res[u][:, 2 * pair : 2 * pair + 2, :]
             nc.scalar.activation(out=res_pair, in_=res_pair, func=ACT.Gelu)
 
-        def store(g, head):
+        def store(u):
+            g, head = divmod(u, HEADS)
             batch, t0 = divmod(g * GROUP, T)
             nc.sync.dma_start(
                 out=out[batch, head, t0 : t0 + GROUP, :].rearrange("(p j) h -> p j h", j=TILES),
-                in_=res[g, head][:],
+                in_=res[u][:],
             )
 
         n_rows = HEADS * D_BLOCKS
@@ -188,7 +205,7 @@ def tile_twostepvoicecraftheads_pa_t_kernel(tc, x, ln_scale, ln_bias, W1, b1, ou
 
         ident = const.tile([P, P], F32)
         make_identity(nc, ident[:])
-        neg_half = const.tile([P, 1], F32)
+        neg_half = const.tile([P, 2], F32)
         nc.vector.memset(neg_half[:], -0.5)
         affine_rows = const.tile([P, P], F32)
         nc.scalar.copy(out=affine_rows[:], in_=affine_rows_bf[:])
@@ -197,10 +214,14 @@ def tile_twostepvoicecraftheads_pa_t_kernel(tc, x, ln_scale, ln_bias, W1, b1, ou
         affine_cols = const.tile([P, P], F32)
         nc.scalar.copy(out=affine_cols[:], in_=affine_cols_ps[:])
 
-        for n in range(STAT_LEAD):
-            normalise(n // TILES, n % TILES)
-        for t in range(PACK):
-            transpose(0, t)
+        for m in range(STAT_LEAD):
+            sum_tokens(m)
+            mean_and_rstd(m)
+            if m < NORM_LEAD:
+                normalise(m)
+            if m == PAIRS - 1:
+                for t in range(PACK):
+                    transpose(0, t)
         w_codes = const.tile([P, HEADS, PASSES * H], U32, align_bytes=64)
         w_scales = const.tile([P, HEADS, PASSES * H], U8, align_bytes=64)
         for head in range(HEADS):
@@ -209,25 +230,40 @@ def tile_twostepvoicecraftheads_pa_t_kernel(tc, x, ln_scale, ln_bias, W1, b1, ou
                 regroup(nc, w_grouped[:, c], w_raw[head][:, c * PACK : (c + 1) * PACK, :])
             quantise(nc, w_codes[:, head, :], w_scales[:, head, :], w_grouped[:].rearrange("p c h t -> p (c h) t"))
 
-        for rnd in range(ROUNDS + GELU_LAG):
-            step, part = divmod(rnd, STEP_ROUNDS)
-            if 1 <= rnd <= ROUNDS:
-                last_step, last_part = divmod(rnd - 1, STEP_ROUNDS)
-                pack(last_step, range(last_part * ROUND_HEADS, (last_part + 1) * ROUND_HEADS))
-            n = rnd + STAT_LEAD
-            if n < GROUPS * TILES:
-                if n % TILES == 0 and n // TILES + 1 < GROUPS:
-                    load(n // TILES + 1)
-                normalise(n // TILES, n % TILES)
-            if 0 <= rnd - PROJECT_LAG < GROUPS * HEADS:
-                project((rnd - PROJECT_LAG) // HEADS, (rnd - PROJECT_LAG) % HEADS)
-            for t in range(PACK):
-                if rnd < ROUNDS:
-                    for head in range(part * ROUND_HEADS, (part + 1) * ROUND_HEADS):
+        for step in range(STEPS + 3):
+            units = [u for u in (2 * (step - 2), 2 * (step - 2) + 1) if 0 <= u < GROUPS * HEADS]
+            for u in units:
+                project(u)
+            if step < STEPS:
+                for t in range(PACK):
+                    for head in FIRST_HEADS:
                         affine(step, t, head)
-                    if part == STEP_ROUNDS - 1 and step + 1 < STEPS:
+            if 1 <= step <= STEPS:
+                pack(step - 1, LAST_HEADS)
+            if step < STEPS:
+                pack(step, FIRST_HEADS)
+
+            if step + NORM_LEAD < GROUPS * PAIRS:
+                normalise(step + NORM_LEAD)
+            if step + STAT_LEAD < GROUPS * PAIRS:
+                if (step + STAT_LEAD) % PAIRS == 0 and (step + STAT_LEAD) // PAIRS + 1 < GROUPS:
+                    load((step + STAT_LEAD) // PAIRS + 1)
+                sum_tokens(step + STAT_LEAD)
+            for u in units[:1]:
+                add_bias(u)
+            if step + STAT_LEAD < GROUPS * PAIRS:
+                mean_and_rstd(step + STAT_LEAD)
+            for u in units[1:]:
+                add_bias(u)
+
+            for t in range(PACK):
+                if step < STEPS:
+                    for head in LAST_HEADS:
+                        affine(step, t, head)
+                    if step + 1 < STEPS:
                         transpose(step + 1, t)
-                if t % 2 == 1 and 0 <= rnd - GELU_LAG < GROUPS * HEADS:
-                    gelu((rnd - GELU_LAG) // HEADS, (rnd - GELU_LAG) % HEADS, t // 2)
-            if 0 <= rnd - GELU_LAG < GROUPS * HEADS:
-                store((rnd - GELU_LAG) // HEADS, (rnd - GELU_LAG) % HEADS)
+                u = 2 * (step - 3) + t // PAIRS
+                if 0 <= u < GROUPS * HEADS:
+                    gelu(u, t % PAIRS)
+                    if t % PAIRS == PAIRS - 1:
+                        store(u)

@@ -24,6 +24,7 @@ D_BLOCKS = D // P
 TILES = 4
 GROUP = TILES * P
 GROUPS = B * T // GROUP
+SCALAR_W = {-1: ((0, 0), (0, 1)), 0: (1, 0), 1: (1, 1)}
 BN_CHUNK = 512
 BN_CHUNKS = D // BN_CHUNK
 BN_DIM = 6
@@ -67,13 +68,27 @@ def tile_twostepvoicecraftheads_pa_t_kernel(tc, x, ln_scale, ln_bias, W1, b1, ou
         xt_psum = ctx.enter_context(tc.psum_pool(name="xt_psum", bufs=PACK))
         acc_psum = ctx.enter_context(tc.psum_pool(name="acc_psum", bufs=2 * PAIRS))
 
+        neg_mean, shift = {}, {}
         x_sb, stats, mean_var, rstd, xn, xt, planes, y_codes, y_scales, acc, res = {}, {}, {}, {}, {}, {}, {}, {}, {}, {}, {}
 
         def load(g):
             x_sb[g] = x_pool.tile([P, TILES, D], BF16, name="x_sb")
             rows = x_rows[g * GROUP : (g + 1) * GROUP, :].rearrange("(p j) d -> p j d", j=TILES)
             for j in range(TILES):
-                nc.sync.dma_start(out=x_sb[g][:, j, :], in_=rows[:, j, :])
+                pieces = BN_CHUNKS if g == 0 and j == 0 else 1
+                for i in range(pieces):
+                    cols = slice(i * D // pieces, (i + 1) * D // pieces)
+                    nc.sync.dma_start(out=x_sb[g][:, j, cols], in_=rows[:, j, cols])
+                if g < PAIRS:
+                    load_weights(*divmod(TILES * g + j, PASSES))
+
+        def load_weights(head, c):
+            if c == 0:
+                w_raw[head] = w_stage.tile([P, D_BLOCKS, H], BF16, name="w_raw", bufs=HEADS)
+            blocks = slice(c * PACK, (c + 1) * PACK)
+            nc.sync.dma_start(
+                out=w_raw[head][:, blocks, :], in_=W1[head].rearrange("(j p) h -> p j h", p=P)[:, blocks, :]
+            )
 
         def sum_tokens(m):
             g, pair = divmod(m, PAIRS)
@@ -96,22 +111,53 @@ def tile_twostepvoicecraftheads_pa_t_kernel(tc, x, ln_scale, ln_bias, W1, b1, ou
             rstd[m] = stat_pool.tile([P, 2], F32, name="rstd")
             nc.gpsimd.tensor_tensor(out=rstd[m][:], in0=var_eps[:], in1=neg_half[:], op=ALU.pow)
 
+        def negate_mean(m):
+            neg_mean[m] = stat_pool.tile([P, 2], F32, name="neg_mean")
+            nc.vector.tensor_scalar_mul(out=neg_mean[m][:], in0=mean_var[m][:, :, 0], scalar1=-1.0)
+
+        def normalise_tile(m, half, cols):
+            g, pair = divmod(m, PAIRS)
+            j = 2 * pair + half
+            nc.gpsimd.tensor_scalar(
+                out=xn[g][:, j, cols],
+                in0=x_sb[g][:, j, cols],
+                scalar1=neg_mean[m][:, half : half + 1],
+                scalar2=rstd[m][:, half : half + 1],
+                op0=ALU.add,
+                op1=ALU.mult,
+            )
+
+        def normalise_tile_on_scalar(m, half, cols):
+            g, pair = divmod(m, PAIRS)
+            j = 2 * pair + half
+            nc.scalar.activation(
+                out=xn[g][:, j, cols],
+                in_=x_sb[g][:, j, cols],
+                func=ACT.Identity,
+                scale=rstd[m][:, half : half + 1],
+                bias=shift[m][:, half : half + 1],
+            )
+
         def normalise(m):
             g, pair = divmod(m, PAIRS)
             if pair == 0:
                 xn[g] = xn_pool.tile([P, TILES, D], F32, name="xn")
-            neg_mean = stat_pool.tile([P, 2], F32)
-            nc.vector.tensor_scalar_mul(out=neg_mean[:], in0=mean_var[m][:, :, 0], scalar1=-1.0)
+            negate_mean(m)
             for half in range(2):
-                j = 2 * pair + half
-                nc.gpsimd.tensor_scalar(
-                    out=xn[g][:, j, :],
-                    in0=x_sb[g][:, j, :],
-                    scalar1=neg_mean[:, half : half + 1],
-                    scalar2=rstd[m][:, half : half + 1],
-                    op0=ALU.add,
-                    op1=ALU.mult,
-                )
+                normalise_tile(m, half, slice(0, D))
+
+        def normalise_first(m):
+            g, pair = divmod(m, PAIRS)
+            if pair == 0:
+                xn[g] = xn_pool.tile([P, TILES, D], F32, name="xn")
+            negate_mean(m)
+            shift[m] = stat_pool.tile([P, 2], F32, name="shift")
+            nc.gpsimd.tensor_tensor(out=shift[m][:], in0=neg_mean[m][:], in1=rstd[m][:], op=ALU.mult)
+            for cols in (slice(0, D // 2), slice(D // 2, D)):
+                normalise_tile(m, 0, cols)
+                normalise_tile_on_scalar(m, 1, cols)
+            if m in SCALAR_W:
+                group_weights_on_scalar(*SCALAR_W[m])
 
         def transpose(step, t):
             g, c = divmod(step, PASSES)
@@ -177,25 +223,23 @@ def tile_twostepvoicecraftheads_pa_t_kernel(tc, x, ln_scale, ln_bias, W1, b1, ou
             res_pair = res[u][:, 2 * pair : 2 * pair + 2, :]
             nc.scalar.activation(out=res_pair, in_=res_pair, func=ACT.Gelu)
 
-        def store(u):
+        def store(u, tiles=slice(0, TILES)):
             g, head = divmod(u, HEADS)
             batch, t0 = divmod(g * GROUP, T)
-            nc.sync.dma_start(
-                out=out[batch, head, t0 : t0 + GROUP, :].rearrange("(p j) h -> p j h", j=TILES),
-                in_=res[u][:],
-            )
+            rows = out[batch, head, t0 : t0 + GROUP, :].rearrange("(p j) h -> p j h", j=TILES)
+            nc.sync.dma_start(out=rows[:, tiles, :], in_=res[u][:, tiles, :])
 
         n_rows = HEADS * D_BLOCKS
+        warm = const.tile([P, 1], F32)
+        nc.vector.memset(warm[:], 0.0)
+        nc.scalar.activation(out=warm[:], in_=warm[:], func=ACT.Gelu)
         affine_rows_bf = const.tile([P, P], BF16)
         nc.vector.memset(affine_rows_bf[:], 0.0)
         nc.scalar.dma_start(out=affine_rows_bf[0:n_rows, :], in_=ln_scale.rearrange("k (j p) -> (k j) p", p=P))
         nc.scalar.dma_start(out=affine_rows_bf[n_rows : 2 * n_rows, :], in_=ln_bias.rearrange("k (j p) -> (k j) p", p=P))
+        w_raw = {}
         load(0)
         load(1)
-        w_raw = {}
-        for head in range(HEADS):
-            w_raw[head] = w_stage.tile([P, D_BLOCKS, H], BF16, name="w_raw", bufs=HEADS)
-            nc.sync.dma_start(out=w_raw[head][:], in_=W1[head].rearrange("(j p) h -> p j h", p=P))
         load(2)
         b1_all = const.tile([P, HEADS, H], BF16)
         nc.scalar.dma_start(
@@ -203,12 +247,24 @@ def tile_twostepvoicecraftheads_pa_t_kernel(tc, x, ln_scale, ln_bias, W1, b1, ou
             in_=b1.rearrange("k h -> (k h)").partition_broadcast(P),
         )
 
+        w_grouped = {}
+
+        def group_weights_on_scalar(head, c):
+            if c == 0:
+                w_grouped[head] = w_stage.tile([P, PASSES, H, PACK], BF16, align_bytes=64, name="w_grouped")
+            nc.scalar.copy(
+                out=w_grouped[head][:, c].rearrange("p (a i) t -> p a t i", i=4),
+                in_=w_raw[head][:, c * PACK : (c + 1) * PACK, :].rearrange("p t (a i) -> p a t i", i=4),
+            )
+
         ident = const.tile([P, P], F32)
         make_identity(nc, ident[:])
         neg_half = const.tile([P, 2], F32)
         nc.vector.memset(neg_half[:], -0.5)
         affine_rows = const.tile([P, P], F32)
         nc.scalar.copy(out=affine_rows[:], in_=affine_rows_bf[:])
+        for head, c in SCALAR_W[-1]:
+            group_weights_on_scalar(head, c)
         affine_cols_ps = xt_psum.tile([P, P], F32, tag="xt")
         nc.tensor.transpose(affine_cols_ps[:], affine_rows[:], ident[:])
         affine_cols = const.tile([P, P], F32)
@@ -217,31 +273,39 @@ def tile_twostepvoicecraftheads_pa_t_kernel(tc, x, ln_scale, ln_bias, W1, b1, ou
         for m in range(STAT_LEAD):
             sum_tokens(m)
             mean_and_rstd(m)
-            if m < NORM_LEAD:
+            if m < PAIRS:
+                normalise_first(m)
+            elif m < NORM_LEAD:
                 normalise(m)
             if m == PAIRS - 1:
                 for t in range(PACK):
                     transpose(0, t)
         w_codes = const.tile([P, HEADS, PASSES * H], U32, align_bytes=64)
         w_scales = const.tile([P, HEADS, PASSES * H], U8, align_bytes=64)
-        for head in range(HEADS):
-            w_grouped = w_stage.tile([P, PASSES, H, PACK], BF16, align_bytes=64)
-            for c in range(PASSES):
-                regroup(nc, w_grouped[:, c], w_raw[head][:, c * PACK : (c + 1) * PACK, :])
-            quantise(nc, w_codes[:, head, :], w_scales[:, head, :], w_grouped[:].rearrange("p c h t -> p (c h) t"))
+        def prepare_weights(head):
+            if head not in w_grouped:
+                w_grouped[head] = w_stage.tile([P, PASSES, H, PACK], BF16, align_bytes=64, name="w_grouped")
+                for c in range(PASSES):
+                    regroup(nc, w_grouped[head][:, c], w_raw[head][:, c * PACK : (c + 1) * PACK, :])
+            quantise(
+                nc, w_codes[:, head, :], w_scales[:, head, :], w_grouped[head][:].rearrange("p c h t -> p (c h) t")
+            )
 
         for step in range(STEPS + 3):
             units = [u for u in (2 * (step - 2), 2 * (step - 2) + 1) if 0 <= u < GROUPS * HEADS]
-            for u in units:
-                project(u)
             if step < STEPS:
                 for t in range(PACK):
                     for head in FIRST_HEADS:
                         affine(step, t, head)
+            if step == 0:
+                for head in range(HEADS):
+                    prepare_weights(head)
             if 1 <= step <= STEPS:
                 pack(step - 1, LAST_HEADS)
             if step < STEPS:
                 pack(step, FIRST_HEADS)
+            for u in units:
+                project(u)
 
             if step + NORM_LEAD < GROUPS * PAIRS:
                 normalise(step + NORM_LEAD)
@@ -257,13 +321,17 @@ def tile_twostepvoicecraftheads_pa_t_kernel(tc, x, ln_scale, ln_bias, W1, b1, ou
                 add_bias(u)
 
             for t in range(PACK):
-                if step < STEPS:
+                if step + 1 < STEPS:
                     for head in LAST_HEADS:
                         affine(step, t, head)
-                    if step + 1 < STEPS:
-                        transpose(step + 1, t)
+                    transpose(step + 1, t)
+                elif step < STEPS:
+                    for k in range(2):
+                        affine(step, (2 * t + k) % PACK, LAST_HEADS[t // 2])
                 u = 2 * (step - 3) + t // PAIRS
                 if 0 <= u < GROUPS * HEADS:
                     gelu(u, t % PAIRS)
-                    if t % PAIRS == PAIRS - 1:
+                    if u == GROUPS * HEADS - 1:
+                        store(u, slice(2 * (t % PAIRS), 2 * (t % PAIRS) + 2))
+                    elif t % PAIRS == PAIRS - 1:
                         store(u)

@@ -24,7 +24,6 @@ D_BLOCKS = D // P
 TILES = 4
 GROUP = TILES * P
 GROUPS = B * T // GROUP
-SCALAR_W = {-1: ((0, 0), (0, 1)), 0: (1, 0), 1: (1, 1)}
 BN_CHUNK = 512
 BN_CHUNKS = D // BN_CHUNK
 BN_DIM = 6
@@ -79,16 +78,10 @@ def tile_twostepvoicecraftheads_pa_t_kernel(tc, x, ln_scale, ln_bias, W1, b1, ou
                 for i in range(pieces):
                     cols = slice(i * D // pieces, (i + 1) * D // pieces)
                     nc.sync.dma_start(out=x_sb[g][:, j, cols], in_=rows[:, j, cols])
-                if g < PAIRS:
-                    load_weights(*divmod(TILES * g + j, PASSES))
 
-        def load_weights(head, c):
-            if c == 0:
-                w_raw[head] = w_stage.tile([P, D_BLOCKS, H], BF16, name="w_raw", bufs=HEADS)
-            blocks = slice(c * PACK, (c + 1) * PACK)
-            nc.sync.dma_start(
-                out=w_raw[head][:, blocks, :], in_=W1[head].rearrange("(j p) h -> p j h", p=P)[:, blocks, :]
-            )
+        def load_weights(head):
+            w_raw[head] = w_stage.tile([P, D_BLOCKS, H], BF16, name="w_raw", bufs=HEADS)
+            nc.sync.dma_start(out=w_raw[head][:], in_=W1[head].rearrange("(j p) h -> p j h", p=P))
 
         def sum_tokens(m):
             g, pair = divmod(m, PAIRS)
@@ -146,6 +139,21 @@ def tile_twostepvoicecraftheads_pa_t_kernel(tc, x, ln_scale, ln_bias, W1, b1, ou
             for half in range(2):
                 normalise_tile(m, half, slice(0, D))
 
+        def normalise_on_vector(m):
+            g, pair = divmod(m, PAIRS)
+            if pair == 0:
+                xn[g] = xn_pool.tile([P, TILES, D], F32, name="xn")
+            for half in range(2):
+                j = 2 * pair + half
+                nc.vector.tensor_scalar(
+                    out=xn[g][:, j, :],
+                    in0=x_sb[g][:, j, :],
+                    scalar1=neg_mean[m][:, half : half + 1],
+                    scalar2=rstd[m][:, half : half + 1],
+                    op0=ALU.add,
+                    op1=ALU.mult,
+                )
+
         def normalise_first(m):
             g, pair = divmod(m, PAIRS)
             if pair == 0:
@@ -156,8 +164,6 @@ def tile_twostepvoicecraftheads_pa_t_kernel(tc, x, ln_scale, ln_bias, W1, b1, ou
             for cols in (slice(0, D // 2), slice(D // 2, D)):
                 normalise_tile(m, 0, cols)
                 normalise_tile_on_scalar(m, 1, cols)
-            if m in SCALAR_W:
-                group_weights_on_scalar(*SCALAR_W[m])
 
         def transpose(step, t):
             g, c = divmod(step, PASSES)
@@ -240,6 +246,8 @@ def tile_twostepvoicecraftheads_pa_t_kernel(tc, x, ln_scale, ln_bias, W1, b1, ou
         w_raw = {}
         load(0)
         load(1)
+        for head in range(HEADS):
+            load_weights(head)
         load(2)
         b1_all = const.tile([P, HEADS, H], BF16)
         nc.scalar.dma_start(
@@ -247,24 +255,12 @@ def tile_twostepvoicecraftheads_pa_t_kernel(tc, x, ln_scale, ln_bias, W1, b1, ou
             in_=b1.rearrange("k h -> (k h)").partition_broadcast(P),
         )
 
-        w_grouped = {}
-
-        def group_weights_on_scalar(head, c):
-            if c == 0:
-                w_grouped[head] = w_stage.tile([P, PASSES, H, PACK], BF16, align_bytes=64, name="w_grouped")
-            nc.scalar.copy(
-                out=w_grouped[head][:, c].rearrange("p (a i) t -> p a t i", i=4),
-                in_=w_raw[head][:, c * PACK : (c + 1) * PACK, :].rearrange("p t (a i) -> p a t i", i=4),
-            )
-
         ident = const.tile([P, P], F32)
         make_identity(nc, ident[:])
         neg_half = const.tile([P, 2], F32)
         nc.vector.memset(neg_half[:], -0.5)
         affine_rows = const.tile([P, P], F32)
         nc.scalar.copy(out=affine_rows[:], in_=affine_rows_bf[:])
-        for head, c in SCALAR_W[-1]:
-            group_weights_on_scalar(head, c)
         affine_cols_ps = xt_psum.tile([P, P], F32, tag="xt")
         nc.tensor.transpose(affine_cols_ps[:], affine_rows[:], ident[:])
         affine_cols = const.tile([P, P], F32)
@@ -276,20 +272,20 @@ def tile_twostepvoicecraftheads_pa_t_kernel(tc, x, ln_scale, ln_bias, W1, b1, ou
             if m < PAIRS:
                 normalise_first(m)
             elif m < NORM_LEAD:
-                normalise(m)
+                negate_mean(m)
             if m == PAIRS - 1:
                 for t in range(PACK):
                     transpose(0, t)
         w_codes = const.tile([P, HEADS, PASSES * H], U32, align_bytes=64)
         w_scales = const.tile([P, HEADS, PASSES * H], U8, align_bytes=64)
+        for m in range(PAIRS, NORM_LEAD):
+            normalise_on_vector(m)
+
         def prepare_weights(head):
-            if head not in w_grouped:
-                w_grouped[head] = w_stage.tile([P, PASSES, H, PACK], BF16, align_bytes=64, name="w_grouped")
-                for c in range(PASSES):
-                    regroup(nc, w_grouped[head][:, c], w_raw[head][:, c * PACK : (c + 1) * PACK, :])
-            quantise(
-                nc, w_codes[:, head, :], w_scales[:, head, :], w_grouped[head][:].rearrange("p c h t -> p (c h) t")
-            )
+            w_grouped = w_stage.tile([P, PASSES, H, PACK], BF16, align_bytes=64, name="w_grouped")
+            for c in range(PASSES):
+                regroup(nc, w_grouped[:, c], w_raw[head][:, c * PACK : (c + 1) * PACK, :])
+            quantise(nc, w_codes[:, head, :], w_scales[:, head, :], w_grouped[:].rearrange("p c h t -> p (c h) t"))
 
         for step in range(STEPS + 3):
             units = [u for u in (2 * (step - 2), 2 * (step - 2) + 1) if 0 <= u < GROUPS * HEADS]
@@ -297,9 +293,8 @@ def tile_twostepvoicecraftheads_pa_t_kernel(tc, x, ln_scale, ln_bias, W1, b1, ou
                 for t in range(PACK):
                     for head in FIRST_HEADS:
                         affine(step, t, head)
-            if step == 0:
-                for head in range(HEADS):
-                    prepare_weights(head)
+            if step < HEADS:
+                prepare_weights(step)
             if 1 <= step <= STEPS:
                 pack(step - 1, LAST_HEADS)
             if step < STEPS:

@@ -40,8 +40,8 @@ FLOPS = 2 * B * HEADS * T * D * H
 
 def regroup(nc, grouped, planes):
     nc.vector.tensor_copy(
-        out=grouped.rearrange("p (a i) t -> p a t i", i=4),
-        in_=planes.rearrange("p t (a i) -> p a t i", i=4),
+        out=grouped.rearrange("p (a i) t -> p a t i", i=8),
+        in_=planes.rearrange("p t (a i) -> p a t i", i=8),
     )
 
 

@@ -24,6 +24,7 @@ D_BLOCKS = D // P
 TILES = 4
 GROUP = TILES * P
 GROUPS = B * T // GROUP
+W_ON_VECTOR, W_LEAD = 2, 2
 BN_CHUNK = 512
 BN_CHUNKS = D // BN_CHUNK
 BN_DIM = 6
@@ -34,6 +35,8 @@ FIRST_HEADS = (0, 1)
 LAST_HEADS = (2, 3)
 NORM_LEAD = 3
 STAT_LEAD = NORM_LEAD + 1
+
+FIRST_HALF, SECOND_HALF = slice(0, D // 2), slice(D // 2, D)
 
 FLOPS = 2 * B * HEADS * T * D * H
 
@@ -161,9 +164,10 @@ def tile_twostepvoicecraftheads_pa_t_kernel(tc, x, ln_scale, ln_bias, W1, b1, ou
             negate_mean(m)
             shift[m] = stat_pool.tile([P, 2], F32, name="shift")
             nc.gpsimd.tensor_tensor(out=shift[m][:], in0=neg_mean[m][:], in1=rstd[m][:], op=ALU.mult)
-            for cols in (slice(0, D // 2), slice(D // 2, D)):
-                normalise_tile(m, 0, cols)
-                normalise_tile_on_scalar(m, 1, cols)
+            normalise_tile(m, 0, FIRST_HALF)
+            normalise_tile_on_scalar(m, 1, FIRST_HALF)
+            if m == 0:
+                normalise_tile_on_scalar(m, 1, SECOND_HALF)
 
         def transpose(step, t):
             g, c = divmod(step, PASSES)
@@ -225,9 +229,8 @@ def tile_twostepvoicecraftheads_pa_t_kernel(tc, x, ln_scale, ln_bias, W1, b1, ou
                     op=ALU.add,
                 )
 
-        def gelu(u, pair):
-            res_pair = res[u][:, 2 * pair : 2 * pair + 2, :]
-            nc.scalar.activation(out=res_pair, in_=res_pair, func=ACT.Gelu)
+        def gelu(u, tiles=slice(0, TILES)):
+            nc.scalar.activation(out=res[u][:, tiles, :], in_=res[u][:, tiles, :], func=ACT.Gelu)
 
         def store(u, tiles=slice(0, TILES)):
             g, head = divmod(u, HEADS)
@@ -276,16 +279,30 @@ def tile_twostepvoicecraftheads_pa_t_kernel(tc, x, ln_scale, ln_bias, W1, b1, ou
             if m == PAIRS - 1:
                 for t in range(PACK):
                     transpose(0, t)
+                for pair in range(PAIRS):
+                    normalise_tile(pair, 0, SECOND_HALF)
+            if m == PAIRS:
+                normalise_tile(PAIRS - 1, 1, SECOND_HALF)
         w_codes = const.tile([P, HEADS, PASSES * H], U32, align_bytes=64)
         w_scales = const.tile([P, HEADS, PASSES * H], U8, align_bytes=64)
         for m in range(PAIRS, NORM_LEAD):
             normalise_on_vector(m)
 
-        def prepare_weights(head):
-            w_grouped = w_stage.tile([P, PASSES, H, PACK], BF16, align_bytes=64, name="w_grouped")
+        w_grouped = {}
+
+        def group_weights(head, on_scalar):
+            w_grouped[head] = w_stage.tile([P, PASSES, H, PACK], BF16, align_bytes=64, name="w_grouped")
             for c in range(PASSES):
-                regroup(nc, w_grouped[:, c], w_raw[head][:, c * PACK : (c + 1) * PACK, :])
-            quantise(nc, w_codes[:, head, :], w_scales[:, head, :], w_grouped[:].rearrange("p c h t -> p (c h) t"))
+                raw = w_raw[head][:, c * PACK : (c + 1) * PACK, :]
+                if on_scalar:
+                    nc.scalar.copy(out=w_grouped[head][:, c], in_=raw.rearrange("p t w -> p w t"))
+                else:
+                    regroup(nc, w_grouped[head][:, c], raw)
+
+        def prepare_weights(head):
+            quantise(
+                nc, w_codes[:, head, :], w_scales[:, head, :], w_grouped[head][:].rearrange("p c h t -> p (c h) t")
+            )
 
         for step in range(STEPS + 3):
             units = [u for u in (2 * (step - 2), 2 * (step - 2) + 1) if 0 <= u < GROUPS * HEADS]
@@ -294,6 +311,8 @@ def tile_twostepvoicecraftheads_pa_t_kernel(tc, x, ln_scale, ln_bias, W1, b1, ou
                     for head in FIRST_HEADS:
                         affine(step, t, head)
             if step < HEADS:
+                if step < W_ON_VECTOR:
+                    group_weights(step, on_scalar=False)
                 prepare_weights(step)
             if 1 <= step <= STEPS:
                 pack(step - 1, LAST_HEADS)
@@ -324,9 +343,12 @@ def tile_twostepvoicecraftheads_pa_t_kernel(tc, x, ln_scale, ln_bias, W1, b1, ou
                     for k in range(2):
                         affine(step, (2 * t + k) % PACK, LAST_HEADS[t // 2])
                 u = 2 * (step - 3) + t // PAIRS
-                if 0 <= u < GROUPS * HEADS:
-                    gelu(u, t % PAIRS)
-                    if u == GROUPS * HEADS - 1:
-                        store(u, slice(2 * (t % PAIRS), 2 * (t % PAIRS) + 2))
-                    elif t % PAIRS == PAIRS - 1:
-                        store(u)
+                if u == GROUPS * HEADS - 1:
+                    tiles = slice(2 * (t % PAIRS), 2 * (t % PAIRS) + 2)
+                    gelu(u, tiles)
+                    store(u, tiles)
+                elif t % PAIRS == PAIRS - 1 and 0 <= u < GROUPS * HEADS:
+                    gelu(u)
+                    store(u)
+            if W_ON_VECTOR <= step + W_LEAD < HEADS:
+                group_weights(step + W_LEAD, on_scalar=True)

from contextlib import ExitStack

import concourse.mybir as mybir
from concourse.masks import make_identity

F32 = mybir.dt.float32
BF16 = mybir.dt.bfloat16
U32 = mybir.dt.uint32
U8 = mybir.dt.uint8
FP8X4 = mybir.dt.float8_e4m3fn_x4
ACT = mybir.ActivationFunctionType
ALU = mybir.AluOpType

HEADS = 4
D = 1024
H = 256
B = 4
T = 1024
LN_EPS = 1e-5
P = 128
PACK = 4
PASSES = D // (P * PACK)
D_BLOCKS = D // P
TILES = 4
GROUP = TILES * P
GROUPS = B * T // GROUP
W_ON_VECTOR, W_LEAD = 2, 2
BN_CHUNK = 512
BN_CHUNKS = D // BN_CHUNK
BN_DIM = 6

STEPS = GROUPS * PASSES
PAIRS = TILES // 2
FIRST_HEADS = (0, 1)
LAST_HEADS = (2, 3)
NORM_LEAD = 3
STAT_LEAD = NORM_LEAD + 1

FIRST_HALF, SECOND_HALF = slice(0, D // 2), slice(D // 2, D)

FLOPS = 2 * B * HEADS * T * D * H


def regroup(nc, grouped, planes):
    nc.vector.tensor_copy(
        out=grouped.rearrange("p (a i) t -> p a t i", i=8),
        in_=planes.rearrange("p t (a i) -> p a t i", i=8),
    )


def quantise(nc, codes, scales, grouped):
    nc.vector.quantize_mx(out=codes.bitcast(FP8X4), scales=scales, in_=grouped.rearrange("p w t -> p (w t)"))


def tile_twostepvoicecraftheads_pa_t_kernel(tc, x, ln_scale, ln_bias, W1, b1, out):
    nc = tc.nc
    x_rows = x.flatten_outer_dims()

    with ExitStack() as ctx:
        ctx.enter_context(tc.manual_schedule())
        const = ctx.enter_context(tc.tile_pool(name="const", bufs=1))
        w_stage = ctx.enter_context(tc.tile_pool(name="w_stage", bufs=2))
        x_pool = ctx.enter_context(tc.tile_pool(name="x_pool", bufs=3))
        xn_pool = ctx.enter_context(tc.tile_pool(name="xn_pool", bufs=2))
        stat_pool = ctx.enter_context(tc.tile_pool(name="stat_pool", bufs=3))
        plane_pool = ctx.enter_context(tc.tile_pool(name="plane_pool", bufs=2 * HEADS))
        grouped_pool = ctx.enter_context(tc.tile_pool(name="grouped_pool", bufs=4))
        y_pool = ctx.enter_context(tc.tile_pool(name="y_pool", bufs=2 * HEADS))
        res_pool = ctx.enter_context(tc.tile_pool(name="res_pool", bufs=6))
        xt_psum = ctx.enter_context(tc.psum_pool(name="xt_psum", bufs=PACK))
        acc_psum = ctx.enter_context(tc.psum_pool(name="acc_psum", bufs=2 * PAIRS))

        neg_mean, shift = {}, {}
        x_sb, stats, mean_var, rstd, xn, xt, planes, y_codes, y_scales, acc, res = {}, {}, {}, {}, {}, {}, {}, {}, {}, {}, {}

        def load(g):
            x_sb[g] = x_pool.tile([P, TILES, D], BF16, name="x_sb")
            rows = x_rows[g * GROUP : (g + 1) * GROUP, :].rearrange("(p j) d -> p j d", j=TILES)
            for j in range(TILES):
                pieces = BN_CHUNKS if g == 0 and j == 0 else 1
                for i in range(pieces):
                    cols = slice(i * D // pieces, (i + 1) * D // pieces)
                    nc.sync.dma_start(out=x_sb[g][:, j, cols], in_=rows[:, j, cols])

        def load_weights(head):
            w_raw[head] = w_stage.tile([P, D_BLOCKS, H], BF16, name="w_raw", bufs=HEADS)
            nc.sync.dma_start(out=w_raw[head][:], in_=W1[head].rearrange("(j p) h -> p j h", p=P))

        def sum_tokens(m):
            g, pair = divmod(m, PAIRS)
            stats[m] = stat_pool.tile([P, 2, BN_CHUNKS * BN_DIM], F32, name="stats")
            for half in range(2):
                for s in range(BN_CHUNKS):
                    nc.vector.bn_stats(
                        out=stats[m][:, half, s * BN_DIM : (s + 1) * BN_DIM],
                        in_=x_sb[g][:, 2 * pair + half, s * BN_CHUNK : (s + 1) * BN_CHUNK],
                    )

        def mean_and_rstd(m):
            mean_var[m] = stat_pool.tile([P, 2, 2], F32, name="mean_var")
            for half in range(2):
                nc.vector.bn_aggr(out=mean_var[m][:, half, :], in_=stats[m][:, half, :])
            var_eps = stat_pool.tile([P, 2], F32)
            nc.gpsimd.tensor_scalar(
                out=var_eps[:], in0=mean_var[m][:, :, 1], scalar1=1.0, scalar2=LN_EPS, op0=ALU.mult, op1=ALU.add
            )
            rstd[m] = stat_pool.tile([P, 2], F32, name="rstd")
            nc.gpsimd.tensor_tensor(out=rstd[m][:], in0=var_eps[:], in1=neg_half[:], op=ALU.pow)

        def negate_mean(m):
            neg_mean[m] = stat_pool.tile([P, 2], F32, name="neg_mean")
            nc.vector.tensor_scalar_mul(out=neg_mean[m][:], in0=mean_var[m][:, :, 0], scalar1=-1.0)

        def normalise_tile(m, half, cols):
            g, pair = divmod(m, PAIRS)
            j = 2 * pair + half
            nc.gpsimd.tensor_scalar(
                out=xn[g][:, j, cols],
                in0=x_sb[g][:, j, cols],
                scalar1=neg_mean[m][:, half : half + 1],
                scalar2=rstd[m][:, half : half + 1],
                op0=ALU.add,
                op1=ALU.mult,
            )

        def normalise_tile_on_scalar(m, half, cols):
            g, pair = divmod(m, PAIRS)
            j = 2 * pair + half
            nc.scalar.activation(
                out=xn[g][:, j, cols],
                in_=x_sb[g][:, j, cols],
                func=ACT.Identity,
                scale=rstd[m][:, half : half + 1],
                bias=shift[m][:, half : half + 1],
            )

        def normalise(m):
            g, pair = divmod(m, PAIRS)
            if pair == 0:
                xn[g] = xn_pool.tile([P, TILES, D], F32, name="xn")
            negate_mean(m)
            for half in range(2):
                normalise_tile(m, half, slice(0, D))

        def normalise_on_vector(m):
            g, pair = divmod(m, PAIRS)
            if pair == 0:
                xn[g] = xn_pool.tile([P, TILES, D], F32, name="xn")
            for half in range(2):
                j = 2 * pair + half
                nc.vector.tensor_scalar(
                    out=xn[g][:, j, :],
                    in0=x_sb[g][:, j, :],
                    scalar1=neg_mean[m][:, half : half + 1],
                    scalar2=rstd[m][:, half : half + 1],
                    op0=ALU.add,
                    op1=ALU.mult,
                )

        def normalise_first(m):
            g, pair = divmod(m, PAIRS)
            if pair == 0:
                xn[g] = xn_pool.tile([P, TILES, D], F32, name="xn")
            negate_mean(m)
            shift[m] = stat_pool.tile([P, 2], F32, name="shift")
            nc.gpsimd.tensor_tensor(out=shift[m][:], in0=neg_mean[m][:], in1=rstd[m][:], op=ALU.mult)
            normalise_tile(m, 0, FIRST_HALF)
            normalise_tile_on_scalar(m, 1, FIRST_HALF)
            if m == 0:
                normalise_tile_on_scalar(m, 1, SECOND_HALF)

        def transpose(step, t):
            g, c = divmod(step, PASSES)
            block = c * PACK + t
            xt[step, t] = xt_psum.tile([P, GROUP], F32, name="xt")
            for j in range(TILES):
                nc.tensor.transpose(
                    xt[step, t][:, j * P : (j + 1) * P], xn[g][:, j, block * P : (block + 1) * P], ident[:]
                )

        def affine(step, t, head):
            if t == 0:
                planes[step, head] = plane_pool.tile([P, PACK, GROUP], BF16, name="planes")
            col = head * D_BLOCKS + (step % PASSES) * PACK + t
            nc.scalar.activation(
                out=planes[step, head][:, t, :],
                in_=xt[step, t][:],
                func=ACT.Identity,
                scale=affine_cols[:, col : col + 1],
                bias=affine_cols[:, n_rows + col : n_rows + col + 1],
            )

        def pack(step, heads):
            g, c = divmod(step, PASSES)
            grouped = {}
            for head in heads:
                if c == 0:
                    y_codes[g, head] = y_pool.tile([P, PASSES, GROUP], U32, align_bytes=64, name="y_codes")
                    y_scales[g, head] = y_pool.tile([P, PASSES, GROUP], U8, align_bytes=64, name="y_scales")
                grouped[head] = grouped_pool.tile([P, GROUP, PACK], BF16, align_bytes=64, name="grouped")
                regroup(nc, grouped[head][:], planes[step, head][:])
            for head in heads:
                quantise(nc, y_codes[g, head][:, c, :], y_scales[g, head][:, c, :], grouped[head][:])

        def project(u):
            g, head = divmod(u, HEADS)
            for pair in range(PAIRS):
                acc[u, pair] = acc_psum.tile([P, 2, H], F32, name="acc")
                for half in range(2):
                    j = 2 * pair + half
                    for c in range(PASSES):
                        nc.tensor.matmul_mx(
                            out=acc[u, pair][:, half, :],
                            lhsT=y_codes[g, head][:, c, j * P : (j + 1) * P].bitcast(FP8X4),
                            lhsT_scale=y_scales[g, head][:, c, j * P : (j + 1) * P],
                            rhs=w_codes[:, head, c * H : (c + 1) * H].bitcast(FP8X4),
                            rhs_scale=w_scales[:, head, c * H : (c + 1) * H],
                            start=(c == 0),
                            stop=(c == PASSES - 1),
                        )

        def add_bias(u):
            res[u] = res_pool.tile([P, TILES, H], F32, name="res")
            for pair in range(PAIRS):
                nc.vector.tensor_tensor(
                    out=res[u][:, 2 * pair : 2 * pair + 2, :],
                    in0=acc[u, pair][:],
                    in1=b1_all[:, u % HEADS, :].unsqueeze(1).to_broadcast([P, 2, H]),
                    op=ALU.add,
                )

        def gelu(u, tiles=slice(0, TILES)):
            nc.scalar.activation(out=res[u][:, tiles, :], in_=res[u][:, tiles, :], func=ACT.Gelu)

        def store(u, tiles=slice(0, TILES)):
            g, head = divmod(u, HEADS)
            batch, t0 = divmod(g * GROUP, T)
            rows = out[batch, head, t0 : t0 + GROUP, :].rearrange("(p j) h -> p j h", j=TILES)
            nc.sync.dma_start(out=rows[:, tiles, :], in_=res[u][:, tiles, :])

        n_rows = HEADS * D_BLOCKS
        warm = const.tile([P, 1], F32)
        nc.vector.memset(warm[:], 0.0)
        nc.scalar.activation(out=warm[:], in_=warm[:], func=ACT.Gelu)
        affine_rows_bf = const.tile([P, P], BF16)
        nc.vector.memset(affine_rows_bf[:], 0.0)
        nc.scalar.dma_start(out=affine_rows_bf[0:n_rows, :], in_=ln_scale.rearrange("k (j p) -> (k j) p", p=P))
        nc.scalar.dma_start(out=affine_rows_bf[n_rows : 2 * n_rows, :], in_=ln_bias.rearrange("k (j p) -> (k j) p", p=P))
        w_raw = {}
        load(0)
        load(1)
        for head in range(HEADS):
            load_weights(head)
        load(2)
        b1_all = const.tile([P, HEADS, H], BF16)
        nc.scalar.dma_start(
            out=b1_all[:].rearrange("p k h -> p (k h)"),
            in_=b1.rearrange("k h -> (k h)").partition_broadcast(P),
        )

        ident = const.tile([P, P], F32)
        make_identity(nc, ident[:])
        neg_half = const.tile([P, 2], F32)
        nc.vector.memset(neg_half[:], -0.5)
        affine_rows = const.tile([P, P], F32)
        nc.scalar.copy(out=affine_rows[:], in_=affine_rows_bf[:])
        affine_cols_ps = xt_psum.tile([P, P], F32, tag="xt")
        nc.tensor.transpose(affine_cols_ps[:], affine_rows[:], ident[:])
        affine_cols = const.tile([P, P], F32)
        nc.scalar.copy(out=affine_cols[:], in_=affine_cols_ps[:])

        for m in range(STAT_LEAD):
            sum_tokens(m)
            mean_and_rstd(m)
            if m < PAIRS:
                normalise_first(m)
            elif m < NORM_LEAD:
                negate_mean(m)
            if m == PAIRS - 1:
                for t in range(PACK):
                    transpose(0, t)
                for pair in range(PAIRS):
                    normalise_tile(pair, 0, SECOND_HALF)
            if m == PAIRS:
                normalise_tile(PAIRS - 1, 1, SECOND_HALF)
        w_codes = const.tile([P, HEADS, PASSES * H], U32, align_bytes=64)
        w_scales = const.tile([P, HEADS, PASSES * H], U8, align_bytes=64)
        for m in range(PAIRS, NORM_LEAD):
            normalise_on_vector(m)

        w_grouped = {}

        def group_weights(head, on_scalar):
            w_grouped[head] = w_stage.tile([P, PASSES, H, PACK], BF16, align_bytes=64, name="w_grouped")
            for c in range(PASSES):
                raw = w_raw[head][:, c * PACK : (c + 1) * PACK, :]
                if on_scalar:
                    nc.scalar.copy(out=w_grouped[head][:, c], in_=raw.rearrange("p t w -> p w t"))
                else:
                    regroup(nc, w_grouped[head][:, c], raw)

        def prepare_weights(head):
            quantise(
                nc, w_codes[:, head, :], w_scales[:, head, :], w_grouped[head][:].rearrange("p c h t -> p (c h) t")
            )

        for step in range(STEPS + 3):
            units = [u for u in (2 * (step - 2), 2 * (step - 2) + 1) if 0 <= u < GROUPS * HEADS]
            if step < STEPS:
                for t in range(PACK):
                    for head in FIRST_HEADS:
                        affine(step, t, head)
            if step < HEADS:
                if step < W_ON_VECTOR:
                    group_weights(step, on_scalar=False)
                prepare_weights(step)
            if 1 <= step <= STEPS:
                pack(step - 1, LAST_HEADS)
            if step < STEPS:
                pack(step, FIRST_HEADS)
            for u in units:
                project(u)

            if step + NORM_LEAD < GROUPS * PAIRS:
                normalise(step + NORM_LEAD)
            if step + STAT_LEAD < GROUPS * PAIRS:
                if (step + STAT_LEAD) % PAIRS == 0 and (step + STAT_LEAD) // PAIRS + 1 < GROUPS:
                    load((step + STAT_LEAD) // PAIRS + 1)
                sum_tokens(step + STAT_LEAD)
            for u in units[:1]:
                add_bias(u)
            if step + STAT_LEAD < GROUPS * PAIRS:
                mean_and_rstd(step + STAT_LEAD)
            for u in units[1:]:
                add_bias(u)

            for t in range(PACK):
                if step + 1 < STEPS:
                    for head in LAST_HEADS:
                        affine(step, t, head)
                    transpose(step + 1, t)
                elif step < STEPS:
                    for k in range(2):
                        affine(step, (2 * t + k) % PACK, LAST_HEADS[t // 2])
                u = 2 * (step - 3) + t // PAIRS
                if u == GROUPS * HEADS - 1:
                    tiles = slice(2 * (t % PAIRS), 2 * (t % PAIRS) + 2)
                    gelu(u, tiles)
                    store(u, tiles)
                elif t % PAIRS == PAIRS - 1 and 0 <= u < GROUPS * HEADS:
                    gelu(u)
                    store(u)
            if W_ON_VECTOR <= step + W_LEAD < HEADS:
                group_weights(step + W_LEAD, on_scalar=True)
